import numpy as np
import ml_dtypes


def mxq(x, axis, fmt="e4m3"):
    dtype, down = {"e4m3": (ml_dtypes.float8_e4m3fn, 7), "e5m2": (ml_dtypes.float8_e5m2, 14)}[fmt]
    v = np.moveaxis(np.asarray(x, np.float32).astype(ml_dtypes.bfloat16).astype(np.float64), axis, -1)
    blocks = v.reshape(v.shape[:-1] + (-1, 32))
    amax = np.abs(blocks).max(-1, keepdims=True)
    byte = np.maximum(np.where(amax > 0, np.frexp(amax)[1] - 1 + 127, 0) - down, 1)
    scale = np.exp2(byte - 127.0)
    codes = (blocks / scale).astype(np.float32).astype(dtype).astype(np.float64)
    return np.moveaxis((codes * scale).reshape(v.shape), -1, axis)


WIDE = False


def mx_kscale(k):
    if not WIDE:
        return np.ones(k)
    levels = np.array([20, -20, 10, -10, 0])
    a = np.random.permutation(np.resize(levels, k // 512 * 4)).reshape(k // 512, 4)
    idx = np.arange(k)
    return np.exp2(a[idx // 512, idx % 128 // 32])


BF16 = ml_dtypes.bfloat16


def bf(x):
    return np.asarray(x, np.float32).astype(BF16)


def f64(x):
    return np.asarray(x).astype(np.float64)


B, D, O, M, R = 2048, 1024, 512, 4, 8
SIGMA = 0.5


def draw(shape, p):
    z = np.random.standard_normal(shape + (R,))
    low = sum(z[..., r:r + 1] * p[r] for r in range(R))
    return 0.6 * low / np.sqrt(R * D) + 0.3 * np.random.standard_normal(shape + (D,)) / np.sqrt(D)


def gauss(x, c):
    x2 = np.sum(x * x, axis=-1)
    c2 = np.sum(c * c, axis=-1)
    xc = (x @ c.reshape(O * M, D).T).reshape(x.shape[0], O, M)
    d = x2[:, None, None] - 2.0 * xc + c2[None, :, :]
    return np.exp(-d / (2.0 * SIGMA * SIGMA))


def setup_inputs():
    basis = np.random.standard_normal((R, D))
    x0 = bf(draw((B,), basis))
    c = bf(draw((O, M), basis))
    g = np.random.standard_normal((B, O)) * np.exp2(np.random.randint(-12, 1, (B, 1))) * 16.0
    probs = gauss(f64(x0), f64(c))
    mx = np.max(probs, axis=-1)
    near = np.sum(probs >= (1.0 - 1e-4) * mx[..., None], axis=-1) > 1
    g = np.where(near, 0.0, g)
    k = mx_kscale(B)
    s = (k / np.min(k))[:, None]
    return {"x": bf(f64(x0) * s), "centers": c, "probs": np.asarray(probs, np.float32), "grad_out": bf(g / s)}


def reference(x, centers, probs, grad_out):
    x, c, p, g = f64(x), f64(centers), f64(probs), f64(grad_out)
    s = np.sum(p, axis=-1)
    mx = np.max(p, axis=-1)
    den = s + M - M * mx
    hot = np.where(p == mx[..., None], 1.0, 0.0)
    dp = (g / (den * den))[..., None] * ((M - M * mx)[..., None] + (M * s)[..., None] * hot)
    w = p * dp / (SIGMA * SIGMA)
    wsum = np.sum(w, axis=0)
    wx = mxq(w.reshape(B, O * M), 0, "e5m2").T @ mxq(x, 0, "e4m3")
    return wx.reshape(O, M, D) - c * wsum[..., None]

@@ -1,0 +1,301 @@
+from contextlib import ExitStack
+
+import concourse.mybir as mybir
+
+F32 = mybir.dt.float32
+BF16 = mybir.dt.bfloat16
+U32 = mybir.dt.uint32
+U8 = mybir.dt.uint8
+E4M3X4 = mybir.dt.float8_e4m3fn_x4
+E5M2X4 = mybir.dt.float8_e5m2_x4
+ALU = mybir.AluOpType
+ACT = mybir.ActivationFunctionType
+
+B, D, O, M = 2048, 1024, 512, 4
+P = 128
+PACK = 4
+K_PASS = P * PACK
+PASSES = B // K_PASS
+ROWS = PASSES * PACK
+O_CHUNK = 64
+COLS = O_CHUNK * M
+CHUNKS = O // O_CHUNK
+GROUPS = ROWS * O_CHUNK
+HALVES = 2
+HALF = GROUPS // HALVES
+M_TILE = 128
+M_TILES = COLS // M_TILE
+N_TILE = 512
+N_TILES = D // N_TILE
+
+FLOPS = 2 * B * O * M * D
+
+
+def tile_pnn_v_kernel(tc, x, centers, probs, grad_out, out):
+    nc = tc.nc
+    centre_rows = centers.rearrange("o m d -> (o m) d")
+    out_rows = out.rearrange("o m d -> (o m) d")
+
+    with ExitStack() as stack:
+        keep = stack.enter_context(tc.tile_pool(name="keep", bufs=1))
+        xstage = stack.enter_context(tc.tile_pool(name="xstage", bufs=2))
+        stream = stack.enter_context(tc.tile_pool(name="stream", bufs=2))
+        small = stack.enter_context(tc.tile_pool(name="small", bufs=1))
+        quant = stack.enter_context(tc.tile_pool(name="quant", bufs=2))
+        result = stack.enter_context(tc.tile_pool(name="result", bufs=4))
+        acc_pool = stack.enter_context(tc.psum_pool(name="acc", bufs=4))
+        sum_pool = stack.enter_context(tc.psum_pool(name="sums", bufs=2))
+        stack.enter_context(tc.manual_schedule())
+
+        one = keep.tile([P, 1], F32)
+        nc.vector.memset(one[:], 1.0)
+        minus_one = keep.tile([P, 1], F32)
+        nc.vector.memset(minus_one[:], -1.0)
+        grad = keep.tile([P, ROWS, O], BF16)
+        x_codes = keep.tile([P, PASSES, D], U32, align_bytes=64)
+        x_scales = keep.tile([P, PASSES, D], U8, align_bytes=64)
+
+        prob = {}
+        centre = {}
+        weight = {}
+        factors = {}
+        codes = {}
+        sums = {}
+        x_tiles = {}
+
+        def load_prob(i):
+            prob[i] = stream.tile([P, PASSES, PACK, COLS], F32, name="prob")
+            for c in range(PASSES):
+                nc.sync.dma_start(
+                    out=prob[i][:, c],
+                    in_=probs[c * K_PASS : (c + 1) * K_PASS, i * O_CHUNK : (i + 1) * O_CHUNK, :].rearrange(
+                        "(p j) o m -> p j (o m)", j=PACK
+                    ),
+                )
+
+        def load_centre(i):
+            centre[i] = stream.tile([P, M_TILES, D], BF16, name="centre")
+            nc.sync.dma_start(
+                out=centre[i][:],
+                in_=centre_rows[i * COLS : (i + 1) * COLS, :].rearrange("(t p) d -> p t d", p=P),
+            )
+
+        def load_grad():
+            for c in range(PASSES):
+                nc.sync.dma_start(
+                    out=grad[:, c * PACK : (c + 1) * PACK, :],
+                    in_=grad_out[c * K_PASS : (c + 1) * K_PASS, :].rearrange("(p j) o -> p j o", j=PACK),
+                )
+
+        def load_x(c):
+            x_raw = xstage.tile([P, PACK, D], BF16, name="x_raw")
+            nc.sync.dma_start(
+                out=x_raw[:], in_=x[c * K_PASS : (c + 1) * K_PASS, :].rearrange("(p j) d -> p j d", j=PACK)
+            )
+            x_tiles[c] = x_raw
+
+        def regroup_x(c):
+            x_grouped = xstage.tile([P, D, PACK], BF16, align_bytes=64, name="x_grouped")
+            nc.scalar.copy(out=x_grouped[:], in_=x_tiles[c][:].rearrange("p j d -> p d j"))
+            x_tiles[c] = x_grouped
+
+        def quantise_x(c):
+            nc.vector.quantize_mx(
+                out=x_codes[:, c, :].bitcast(E4M3X4),
+                scales=x_scales[:, c, :],
+                in_=x_tiles[c][:].rearrange("p d j -> p (d j)"),
+            )
+
+        def by_group(tile_ap):
+            return tile_ap.rearrange("p c j (o m) -> p (c j o) m", m=M)
+
+        def front(i):
+            prob4 = by_group(prob[i][:])
+            pair_max = small.tile([P, GROUPS, 2], F32, name="pair_max")
+            pair_sum = small.tile([P, GROUPS, 2], F32, name="pair_sum")
+            top = small.tile([P, GROUPS, 1], F32, name="top")
+            total = small.tile([P, GROUPS, 1], F32, name="total")
+            den = small.tile([P, GROUPS, 1], F32, name="den")
+            nc.vector.tensor_tensor(out=pair_max[:], in0=prob4[:, :, 0:2], in1=prob4[:, :, 2:4], op=ALU.max)
+            nc.vector.tensor_tensor(out=pair_sum[:], in0=prob4[:, :, 0:2], in1=prob4[:, :, 2:4], op=ALU.add)
+            nc.vector.tensor_tensor(out=top[:], in0=pair_max[:, :, 0:1], in1=pair_max[:, :, 1:2], op=ALU.max)
+            nc.vector.tensor_tensor(out=total[:], in0=pair_sum[:, :, 0:1], in1=pair_sum[:, :, 1:2], op=ALU.add)
+            nc.vector.scalar_tensor_tensor(
+                out=den[:], in0=top[:], scalar=-4.0, in1=total[:], op0=ALU.mult, op1=ALU.add
+            )
+            dsq = small.tile([P, GROUPS, 1], F32, name="dsq")
+            seed = small.tile([P, GROUPS, 1], F32, name="seed")
+            rest = small.tile([P, GROUPS, 1], F32, name="rest")
+            nc.scalar.activation(out=dsq[:], in_=den[:], func=ACT.Square, bias=one[:, 0:1], scale=0.25)
+            nc.scalar.activation(out=seed[:], in_=dsq[:], func=ACT.Square)
+            nc.scalar.activation(out=seed[:], in_=seed[:], func=ACT.Abs_reciprocal_sqrt)
+            nc.scalar.activation(out=rest[:], in_=top[:], func=ACT.Identity, bias=minus_one[:, 0:1], scale=1.0)
+            factors[i] = {"top": top, "total": total, "dsq": dsq, "seed": seed, "rest": rest}
+
+        def mark_top(i):
+            weight[i] = stream.tile([P, PASSES, PACK, COLS], F32, name="weight")
+            nc.vector.tensor_tensor(
+                out=by_group(weight[i][:]),
+                in0=by_group(prob[i][:]),
+                in1=factors[i]["top"][:].to_broadcast([P, GROUPS, M]),
+                op=ALU.is_equal,
+            )
+
+        def make_factors(i):
+            f = factors[i]
+            corr = small.tile([P, GROUPS, 1], F32, name="corr")
+            gain = small.tile([P, GROUPS, 1], F32, name="gain")
+            base = small.tile([P, GROUPS, 1], F32, name="base")
+            bonus = small.tile([P, GROUPS, 1], F32, name="bonus")
+            nc.vector.tensor_tensor(
+                out=gain[:].rearrange("p (r o) u -> p r (o u)", o=O_CHUNK),
+                in0=f["seed"][:].rearrange("p (r o) u -> p r (o u)", o=O_CHUNK),
+                in1=grad[:, :, i * O_CHUNK : (i + 1) * O_CHUNK],
+                op=ALU.mult,
+            )
+            nc.vector.tensor_tensor(out=corr[:], in0=f["dsq"][:], in1=f["seed"][:], op=ALU.mult)
+            nc.vector.scalar_tensor_tensor(
+                out=gain[:], in0=corr[:], scalar=2.0, in1=gain[:], op0=ALU.subtract, op1=ALU.mult
+            )
+            nc.vector.tensor_tensor(out=base[:], in0=f["rest"][:], in1=gain[:], op=ALU.mult)
+            nc.vector.scalar_tensor_tensor(
+                out=bonus[:], in0=f["total"][:], scalar=-1.0, in1=gain[:], op0=ALU.mult, op1=ALU.mult
+            )
+            f["base"] = base
+            f["bonus"] = bonus
+
+        def make_weights(i):
+            weight4 = by_group(weight[i][:])
+            prob4 = by_group(prob[i][:])
+            halves = [slice(h * HALF, (h + 1) * HALF) for h in range(HALVES)]
+            for hs in halves:
+                nc.vector.tensor_tensor(
+                    out=weight4[:, hs, :],
+                    in0=weight4[:, hs, :],
+                    in1=factors[i]["bonus"][:, hs, :].to_broadcast([P, HALF, M]),
+                    op=ALU.mult,
+                )
+            for hs in halves:
+                nc.vector.tensor_tensor(
+                    out=weight4[:, hs, :],
+                    in0=weight4[:, hs, :],
+                    in1=factors[i]["base"][:, hs, :].to_broadcast([P, HALF, M]),
+                    op=ALU.add,
+                )
+            for hs in halves:
+                nc.vector.tensor_tensor(out=weight4[:, hs, :], in0=weight4[:, hs, :], in1=prob4[:, hs, :], op=ALU.mult)
+
+        def regroup(i):
+            grouped = quant.tile([P, PASSES, COLS, PACK], BF16, align_bytes=64, name="grouped")
+            per_half = PASSES // HALVES
+            for h in range(HALVES):
+                cs = slice(h * per_half, (h + 1) * per_half)
+                nc.scalar.copy(out=grouped[:, cs], in_=weight[i][:, cs].rearrange("p c j w -> p c w j"))
+            codes[i] = {"grouped": grouped}
+
+        def column_sums(i):
+            sums[i] = []
+            for t in range(M_TILES):
+                minus_sum_ps = sum_pool.tile([P, 1], F32, name="minus_sum_ps")
+                for r in range(ROWS):
+                    nc.tensor.matmul(
+                        out=minus_sum_ps[:],
+                        lhsT=weight[i][:, r // PACK, r % PACK, t * M_TILE : (t + 1) * M_TILE],
+                        rhs=minus_one[:],
+                        start=(r == 0),
+                        stop=(r == ROWS - 1),
+                    )
+                sums[i].append(minus_sum_ps)
+
+        def quantise(i):
+            w_codes = quant.tile([P, PASSES * COLS], U32, align_bytes=64, name="w_codes")
+            w_scales = quant.tile([P, PASSES * COLS], U8, align_bytes=64, name="w_scales")
+            nc.vector.quantize_mx(
+                out=w_codes[:].bitcast(E5M2X4),
+                scales=w_scales[:],
+                in_=codes[i]["grouped"][:].rearrange("p c w j -> p (c w j)"),
+            )
+            codes[i]["w_codes"] = w_codes
+            codes[i]["w_scales"] = w_scales
+
+        def products(i):
+            w_codes = codes[i]["w_codes"]
+            w_scales = codes[i]["w_scales"]
+            accs = []
+            for t in range(M_TILES):
+                minus_sum = result.tile([P, 1], F32, name="minus_sum")
+                nc.scalar.copy(out=minus_sum[:], in_=sums[i][t][:])
+                sums[i][t] = minus_sum
+                for n in range(N_TILES):
+                    acc = acc_pool.tile([P, N_TILE], F32, name="acc")
+                    for c in range(PASSES):
+                        w_cols = slice(c * COLS + t * M_TILE, c * COLS + (t + 1) * M_TILE)
+                        x_cols = slice(n * N_TILE, (n + 1) * N_TILE)
+                        nc.tensor.matmul_mx(
+                            out=acc[:],
+                            lhsT=w_codes[:, w_cols].bitcast(E5M2X4),
+                            lhsT_scale=w_scales[:, w_cols],
+                            rhs=x_codes[:, c, x_cols].bitcast(E4M3X4),
+                            rhs_scale=x_scales[:, c, x_cols],
+                            start=(c == 0),
+                            stop=(c == PASSES - 1),
+                        )
+                    accs.append(acc)
+            codes[i]["accs"] = accs
+
+        def finish(i):
+            for t in range(M_TILES):
+                for n in range(N_TILES):
+                    res = result.tile([P, N_TILE], F32, name="res")
+                    nc.vector.scalar_tensor_tensor(
+                        out=res[:],
+                        in0=centre[i][:, t, n * N_TILE : (n + 1) * N_TILE],
+                        scalar=sums[i][t][:, 0:1],
+                        in1=codes[i]["accs"][t * N_TILES + n][:],
+                        op0=ALU.mult,
+                        op1=ALU.add,
+                    )
+                    row0 = i * COLS + t * M_TILE
+                    nc.sync.dma_start(
+                        out=out_rows[row0 : row0 + M_TILE, n * N_TILE : (n + 1) * N_TILE], in_=res[:]
+                    )
+
+        load_prob(0)
+        load_grad()
+        load_x(0)
+        load_x(1)
+        load_prob(1)
+        load_centre(0)
+        front(0)
+        mark_top(0)
+        regroup_x(0)
+        regroup_x(1)
+        load_x(2)
+        load_x(3)
+        make_factors(0)
+        for i in range(CHUNKS):
+            if i + 1 < CHUNKS:
+                front(i + 1)
+            if i == 0:
+                quantise_x(0)
+                quantise_x(1)
+                regroup_x(2)
+                regroup_x(3)
+            make_weights(i)
+            if i + 2 < CHUNKS:
+                load_prob(i + 2)
+            regroup(i)
+            column_sums(i)
+            if i + 1 < CHUNKS:
+                mark_top(i + 1)
+                make_factors(i + 1)
+            if i == 0:
+                quantise_x(2)
+                quantise_x(3)
+            if i >= 1:
+                finish(i - 1)
+            if i + 1 < CHUNKS:
+                load_centre(i + 1)
+            quantise(i)
+            products(i)
+        finish(CHUNKS - 1)

@@ -1,6 +1,7 @@
 from contextlib import ExitStack
 
 import concourse.mybir as mybir
+from concourse.masks import make_identity
 
 F32 = mybir.dt.float32
 BF16 = mybir.dt.bfloat16
@@ -44,13 +45,16 @@ def tile_pnn_v_kernel(tc, x, centers, probs, grad_out, out):
         quant = stack.enter_context(tc.tile_pool(name="quant", bufs=2))
         result = stack.enter_context(tc.tile_pool(name="result", bufs=4))
         acc_pool = stack.enter_context(tc.psum_pool(name="acc", bufs=4))
-        sum_pool = stack.enter_context(tc.psum_pool(name="sums", bufs=2))
+        sum_pool = stack.enter_context(tc.psum_pool(name="sums", bufs=1))
+        spread_pool = stack.enter_context(tc.psum_pool(name="spread", bufs=3))
         stack.enter_context(tc.manual_schedule())
 
         one = keep.tile([P, 1], F32)
         nc.vector.memset(one[:], 1.0)
         minus_one = keep.tile([P, 1], F32)
         nc.vector.memset(minus_one[:], -1.0)
+        ident = keep.tile([P, P], F32)
+        make_identity(nc, ident[:])
         grad = keep.tile([P, ROWS, O], BF16)
         x_codes = keep.tile([P, PASSES, D], U32, align_bytes=64)
         x_scales = keep.tile([P, PASSES, D], U8, align_bytes=64)
@@ -132,14 +136,26 @@ def tile_pnn_v_kernel(tc, x, centers, probs, grad_out, out):
             nc.scalar.activation(out=rest[:], in_=top[:], func=ACT.Identity, bias=minus_one[:, 0:1], scale=1.0)
             factors[i] = {"top": top, "total": total, "dsq": dsq, "seed": seed, "rest": rest}
 
-        def mark_top(i):
-            weight[i] = stream.tile([P, PASSES, PACK, COLS], F32, name="weight")
+        def half(h):
+            return slice(h * HALF, (h + 1) * HALF)
+
+        def spread(values, h):
+            bank = spread_pool.tile([P, HALF, 1], F32, name="bank")
+            nc.tensor.matmul(out=bank[:, :, 0], lhsT=ident[:], rhs=values[:, half(h), 0], start=True, stop=True)
+            return bank
+
+        def with_factor(i, h, bank, op, source):
             nc.vector.tensor_tensor(
-                out=by_group(weight[i][:]),
-                in0=by_group(prob[i][:]),
-                in1=factors[i]["top"][:].to_broadcast([P, GROUPS, M]),
-                op=ALU.is_equal,
+                out=by_group(weight[i][:])[:, half(h), :],
+                in0=by_group(source[i][:])[:, half(h), :],
+                in1=bank[:].to_broadcast([P, HALF, M]),
+                op=op,
             )
+
+        def mark_top(i, banks):
+            weight[i] = stream.tile([P, PASSES, PACK, COLS], F32, name="weight")
+            for h in range(HALVES):
+                with_factor(i, h, banks[h], ALU.is_equal, prob)
 
         def make_factors(i):
             f = factors[i]
@@ -164,26 +180,33 @@ def tile_pnn_v_kernel(tc, x, centers, probs, grad_out, out):
             f["base"] = base
             f["bonus"] = bonus
 
-        def make_weights(i):
-            weight4 = by_group(weight[i][:])
-            prob4 = by_group(prob[i][:])
-            halves = [slice(h * HALF, (h + 1) * HALF) for h in range(HALVES)]
-            for hs in halves:
-                nc.vector.tensor_tensor(
-                    out=weight4[:, hs, :],
-                    in0=weight4[:, hs, :],
-                    in1=factors[i]["bonus"][:, hs, :].to_broadcast([P, HALF, M]),
-                    op=ALU.mult,
-                )
-            for hs in halves:
-                nc.vector.tensor_tensor(
-                    out=weight4[:, hs, :],
-                    in0=weight4[:, hs, :],
-                    in1=factors[i]["base"][:, hs, :].to_broadcast([P, HALF, M]),
-                    op=ALU.add,
-                )
-            for hs in halves:
-                nc.vector.tensor_tensor(out=weight4[:, hs, :], in0=weight4[:, hs, :], in1=prob4[:, hs, :], op=ALU.mult)
+        def first_spreads(i):
+            f = factors[i]
+            return [spread(f["bonus"], 0), spread(f["base"], 0), spread(f["bonus"], 1)]
+
+        def last_factor(i, h):
+            nc.gpsimd.tensor_tensor(
+                out=by_group(weight[i][:])[:, half(h), :],
+                in0=by_group(weight[i][:])[:, half(h), :],
+                in1=by_group(prob[i][:])[:, half(h), :],
+                op=ALU.mult,
+            )
+
+        def make_weights(i, banks):
+            bonus_0, base_0, bonus_1 = banks
+            tops = []
+            with_factor(i, 0, bonus_0, ALU.mult, weight)
+            base_1 = spread(factors[i]["base"], 1)
+            with_factor(i, 0, base_0, ALU.add, weight)
+            last_factor(i, 0)
+            if i + 1 < CHUNKS:
+                tops.append(spread(factors[i + 1]["top"], 0))
+            with_factor(i, 1, bonus_1, ALU.mult, weight)
+            if i + 1 < CHUNKS:
+                tops.append(spread(factors[i + 1]["top"], 1))
+            with_factor(i, 1, base_1, ALU.add, weight)
+            last_factor(i, 1)
+            return tops
 
         def regroup(i):
             grouped = quant.tile([P, PASSES, COLS, PACK], BF16, align_bytes=64, name="grouped")
@@ -194,18 +217,17 @@ def tile_pnn_v_kernel(tc, x, centers, probs, grad_out, out):
             codes[i] = {"grouped": grouped}
 
         def column_sums(i):
-            sums[i] = []
+            minus_sum_ps = sum_pool.tile([P, M_TILES], F32, name="minus_sum_ps")
+            sums[i] = minus_sum_ps
             for t in range(M_TILES):
-                minus_sum_ps = sum_pool.tile([P, 1], F32, name="minus_sum_ps")
                 for r in range(ROWS):
                     nc.tensor.matmul(
-                        out=minus_sum_ps[:],
+                        out=minus_sum_ps[:, t : t + 1],
                         lhsT=weight[i][:, r // PACK, r % PACK, t * M_TILE : (t + 1) * M_TILE],
                         rhs=minus_one[:],
                         start=(r == 0),
                         stop=(r == ROWS - 1),
                     )
-                sums[i].append(minus_sum_ps)
 
         def quantise(i):
             w_codes = quant.tile([P, PASSES * COLS], U32, align_bytes=64, name="w_codes")
@@ -222,10 +244,10 @@ def tile_pnn_v_kernel(tc, x, centers, probs, grad_out, out):
             w_codes = codes[i]["w_codes"]
             w_scales = codes[i]["w_scales"]
             accs = []
+            minus_sum = result.tile([P, M_TILES], F32, name="minus_sum")
+            nc.scalar.copy(out=minus_sum[:], in_=sums[i][:])
+            sums[i] = minus_sum
             for t in range(M_TILES):
-                minus_sum = result.tile([P, 1], F32, name="minus_sum")
-                nc.scalar.copy(out=minus_sum[:], in_=sums[i][t][:])
-                sums[i][t] = minus_sum
                 for n in range(N_TILES):
                     acc = acc_pool.tile([P, N_TILE], F32, name="acc")
                     for c in range(PASSES):
@@ -250,7 +272,7 @@ def tile_pnn_v_kernel(tc, x, centers, probs, grad_out, out):
                     nc.vector.scalar_tensor_tensor(
                         out=res[:],
                         in0=centre[i][:, t, n * N_TILE : (n + 1) * N_TILE],
-                        scalar=sums[i][t][:, 0:1],
+                        scalar=sums[i][:, t : t + 1],
                         in1=codes[i]["accs"][t * N_TILES + n][:],
                         op0=ALU.mult,
                         op1=ALU.add,
@@ -267,12 +289,13 @@ def tile_pnn_v_kernel(tc, x, centers, probs, grad_out, out):
         load_prob(1)
         load_centre(0)
         front(0)
-        mark_top(0)
+        mark_top(0, [spread(factors[0]["top"], 0), spread(factors[0]["top"], 1)])
         regroup_x(0)
         regroup_x(1)
         load_x(2)
         load_x(3)
         make_factors(0)
+        banks = first_spreads(0)
         for i in range(CHUNKS):
             if i + 1 < CHUNKS:
                 front(i + 1)
@@ -281,21 +304,22 @@ def tile_pnn_v_kernel(tc, x, centers, probs, grad_out, out):
                 quantise_x(1)
                 regroup_x(2)
                 regroup_x(3)
-            make_weights(i)
+            tops = make_weights(i, banks)
             if i + 2 < CHUNKS:
                 load_prob(i + 2)
             regroup(i)
             column_sums(i)
             if i + 1 < CHUNKS:
-                mark_top(i + 1)
-                make_factors(i + 1)
-            if i == 0:
-                quantise_x(2)
-                quantise_x(3)
+                mark_top(i + 1, tops)
             if i >= 1:
                 finish(i - 1)
             if i + 1 < CHUNKS:
                 load_centre(i + 1)
+                make_factors(i + 1)
+                banks = first_spreads(i + 1)
+            if i == 0:
+                quantise_x(2)
+                quantise_x(3)
             quantise(i)
             products(i)
         finish(CHUNKS - 1)

@@ -40,6 +40,7 @@ def tile_pnn_v_kernel(tc, x, centers, probs, grad_out, out):
     with ExitStack() as stack:
         keep = stack.enter_context(tc.tile_pool(name="keep", bufs=1))
         xstage = stack.enter_context(tc.tile_pool(name="xstage", bufs=2))
+        prob_pool = stack.enter_context(tc.tile_pool(name="prob_pool", bufs=3))
         stream = stack.enter_context(tc.tile_pool(name="stream", bufs=2))
         small = stack.enter_context(tc.tile_pool(name="small", bufs=1))
         quant = stack.enter_context(tc.tile_pool(name="quant", bufs=2))
@@ -55,11 +56,12 @@ def tile_pnn_v_kernel(tc, x, centers, probs, grad_out, out):
         nc.vector.memset(minus_one[:], -1.0)
         ident = keep.tile([P, P], F32)
         make_identity(nc, ident[:])
-        grad = keep.tile([P, ROWS, O], BF16)
         x_codes = keep.tile([P, PASSES, D], U32, align_bytes=64)
         x_scales = keep.tile([P, PASSES, D], U8, align_bytes=64)
 
         prob = {}
+        grad = {}
+        pair_sums = {}
         centre = {}
         weight = {}
         factors = {}
@@ -68,7 +70,7 @@ def tile_pnn_v_kernel(tc, x, centers, probs, grad_out, out):
         x_tiles = {}
 
         def load_prob(i):
-            prob[i] = stream.tile([P, PASSES, PACK, COLS], F32, name="prob")
+            prob[i] = prob_pool.tile([P, PASSES, PACK, COLS], F32, name="prob")
             for c in range(PASSES):
                 nc.sync.dma_start(
                     out=prob[i][:, c],
@@ -84,11 +86,14 @@ def tile_pnn_v_kernel(tc, x, centers, probs, grad_out, out):
                 in_=centre_rows[i * COLS : (i + 1) * COLS, :].rearrange("(t p) d -> p t d", p=P),
             )
 
-        def load_grad():
+        def load_grad(i):
+            grad[i] = stream.tile([P, ROWS, O_CHUNK], BF16, name="grad")
             for c in range(PASSES):
                 nc.sync.dma_start(
-                    out=grad[:, c * PACK : (c + 1) * PACK, :],
-                    in_=grad_out[c * K_PASS : (c + 1) * K_PASS, :].rearrange("(p j) o -> p j o", j=PACK),
+                    out=grad[i][:, c * PACK : (c + 1) * PACK, :],
+                    in_=grad_out[c * K_PASS : (c + 1) * K_PASS, i * O_CHUNK : (i + 1) * O_CHUNK].rearrange(
+                        "(p j) o -> p j o", j=PACK
+                    ),
                 )
 
         def load_x(c):
@@ -113,15 +118,19 @@ def tile_pnn_v_kernel(tc, x, centers, probs, grad_out, out):
         def by_group(tile_ap):
             return tile_ap.rearrange("p c j (o m) -> p (c j o) m", m=M)
 
+        def sum_pairs(i):
+            prob4 = by_group(prob[i][:])
+            pair_sums[i] = small.tile([P, GROUPS, 2], F32, name="pair_sum")
+            nc.gpsimd.tensor_tensor(out=pair_sums[i][:], in0=prob4[:, :, 0:2], in1=prob4[:, :, 2:4], op=ALU.add)
+
         def front(i):
             prob4 = by_group(prob[i][:])
+            pair_sum = pair_sums[i]
             pair_max = small.tile([P, GROUPS, 2], F32, name="pair_max")
-            pair_sum = small.tile([P, GROUPS, 2], F32, name="pair_sum")
             top = small.tile([P, GROUPS, 1], F32, name="top")
             total = small.tile([P, GROUPS, 1], F32, name="total")
-            den = small.tile([P, GROUPS, 1], F32, name="den")
+            den = small.tile([P, GROUPS, 1], F32, name="den", tag="den_then_corr")
             nc.vector.tensor_tensor(out=pair_max[:], in0=prob4[:, :, 0:2], in1=prob4[:, :, 2:4], op=ALU.max)
-            nc.vector.tensor_tensor(out=pair_sum[:], in0=prob4[:, :, 0:2], in1=prob4[:, :, 2:4], op=ALU.add)
             nc.vector.tensor_tensor(out=top[:], in0=pair_max[:, :, 0:1], in1=pair_max[:, :, 1:2], op=ALU.max)
             nc.vector.tensor_tensor(out=total[:], in0=pair_sum[:, :, 0:1], in1=pair_sum[:, :, 1:2], op=ALU.add)
             nc.vector.scalar_tensor_tensor(
@@ -159,14 +168,14 @@ def tile_pnn_v_kernel(tc, x, centers, probs, grad_out, out):
 
         def make_factors(i):
             f = factors[i]
-            corr = small.tile([P, GROUPS, 1], F32, name="corr")
+            corr = small.tile([P, GROUPS, 1], F32, name="corr", tag="den_then_corr")
             gain = small.tile([P, GROUPS, 1], F32, name="gain")
             base = small.tile([P, GROUPS, 1], F32, name="base")
             bonus = small.tile([P, GROUPS, 1], F32, name="bonus")
             nc.vector.tensor_tensor(
                 out=gain[:].rearrange("p (r o) u -> p r (o u)", o=O_CHUNK),
                 in0=f["seed"][:].rearrange("p (r o) u -> p r (o u)", o=O_CHUNK),
-                in1=grad[:, :, i * O_CHUNK : (i + 1) * O_CHUNK],
+                in1=grad[i][:],
                 op=ALU.mult,
             )
             nc.vector.tensor_tensor(out=corr[:], in0=f["dsq"][:], in1=f["seed"][:], op=ALU.mult)
@@ -232,29 +241,31 @@ def tile_pnn_v_kernel(tc, x, centers, probs, grad_out, out):
         def quantise(i):
             w_codes = quant.tile([P, PASSES * COLS], U32, align_bytes=64, name="w_codes")
             w_scales = quant.tile([P, PASSES * COLS], U8, align_bytes=64, name="w_scales")
-            nc.vector.quantize_mx(
-                out=w_codes[:].bitcast(E5M2X4),
-                scales=w_scales[:],
-                in_=codes[i]["grouped"][:].rearrange("p c w j -> p (c w j)"),
-            )
+            words = PASSES * COLS // HALVES
+            per_half = PASSES // HALVES
+            for h in range(HALVES):
+                nc.vector.quantize_mx(
+                    out=w_codes[:, h * words : (h + 1) * words].bitcast(E5M2X4),
+                    scales=w_scales[:, h * words : (h + 1) * words],
+                    in_=codes[i]["grouped"][:, h * per_half : (h + 1) * per_half].rearrange("p c w j -> p (c w j)"),
+                )
             codes[i]["w_codes"] = w_codes
             codes[i]["w_scales"] = w_scales
 
         def products(i):
             w_codes = codes[i]["w_codes"]
             w_scales = codes[i]["w_scales"]
-            accs = []
             minus_sum = result.tile([P, M_TILES], F32, name="minus_sum")
             nc.scalar.copy(out=minus_sum[:], in_=sums[i][:])
             sums[i] = minus_sum
-            for t in range(M_TILES):
-                for n in range(N_TILES):
-                    acc = acc_pool.tile([P, N_TILE], F32, name="acc")
-                    for c in range(PASSES):
+            accs = [acc_pool.tile([P, N_TILE], F32, name="acc") for k in range(M_TILES * N_TILES)]
+            for c in range(PASSES):
+                for t in range(M_TILES):
+                    for n in range(N_TILES):
                         w_cols = slice(c * COLS + t * M_TILE, c * COLS + (t + 1) * M_TILE)
                         x_cols = slice(n * N_TILE, (n + 1) * N_TILE)
                         nc.tensor.matmul_mx(
-                            out=acc[:],
+                            out=accs[t * N_TILES + n][:],
                             lhsT=w_codes[:, w_cols].bitcast(E5M2X4),
                             lhsT_scale=w_scales[:, w_cols],
                             rhs=x_codes[:, c, x_cols].bitcast(E4M3X4),
@@ -262,7 +273,6 @@ def tile_pnn_v_kernel(tc, x, centers, probs, grad_out, out):
                             start=(c == 0),
                             stop=(c == PASSES - 1),
                         )
-                    accs.append(acc)
             codes[i]["accs"] = accs
 
         def finish(i):
@@ -283,30 +293,37 @@ def tile_pnn_v_kernel(tc, x, centers, probs, grad_out, out):
                     )
 
         load_prob(0)
-        load_grad()
+        load_grad(0)
         load_x(0)
         load_x(1)
         load_prob(1)
+        load_grad(1)
         load_centre(0)
+        sum_pairs(0)
         front(0)
+        sum_pairs(1)
         mark_top(0, [spread(factors[0]["top"], 0), spread(factors[0]["top"], 1)])
         regroup_x(0)
         regroup_x(1)
         load_x(2)
         load_x(3)
+        load_prob(2)
         make_factors(0)
         banks = first_spreads(0)
         for i in range(CHUNKS):
             if i + 1 < CHUNKS:
                 front(i + 1)
+            if i + 2 < CHUNKS:
+                sum_pairs(i + 2)
+                load_grad(i + 2)
             if i == 0:
                 quantise_x(0)
                 quantise_x(1)
                 regroup_x(2)
                 regroup_x(3)
             tops = make_weights(i, banks)
-            if i + 2 < CHUNKS:
-                load_prob(i + 2)
+            if i + 3 < CHUNKS:
+                load_prob(i + 3)
             regroup(i)
             column_sums(i)
             if i + 1 < CHUNKS:

@@ -24,10 +24,13 @@ CHUNKS = O // O_CHUNK
 GROUPS = ROWS * O_CHUNK
 HALVES = 2
 HALF = GROUPS // HALVES
+HALF_PASSES = PASSES // HALVES
+HALF_WORDS = HALF_PASSES * COLS
 M_TILE = 128
 M_TILES = COLS // M_TILE
 N_TILE = 512
 N_TILES = D // N_TILE
+OUT_TILES = M_TILES * N_TILES
 
 FLOPS = 2 * B * O * M * D
 
@@ -39,15 +42,15 @@ def tile_pnn_v_kernel(tc, x, centers, probs, grad_out, out):
 
     with ExitStack() as stack:
         keep = stack.enter_context(tc.tile_pool(name="keep", bufs=1))
-        xstage = stack.enter_context(tc.tile_pool(name="xstage", bufs=2))
+        x_stage = stack.enter_context(tc.tile_pool(name="x_stage", bufs=2))
         prob_pool = stack.enter_context(tc.tile_pool(name="prob_pool", bufs=3))
         stream = stack.enter_context(tc.tile_pool(name="stream", bufs=2))
         small = stack.enter_context(tc.tile_pool(name="small", bufs=1))
         quant = stack.enter_context(tc.tile_pool(name="quant", bufs=2))
-        result = stack.enter_context(tc.tile_pool(name="result", bufs=4))
-        acc_pool = stack.enter_context(tc.psum_pool(name="acc", bufs=4))
+        result = stack.enter_context(tc.tile_pool(name="result", bufs=OUT_TILES))
+        acc_pool = stack.enter_context(tc.psum_pool(name="acc", bufs=OUT_TILES))
+        copy_pool = stack.enter_context(tc.psum_pool(name="copies", bufs=3))
         sum_pool = stack.enter_context(tc.psum_pool(name="sums", bufs=1))
-        spread_pool = stack.enter_context(tc.psum_pool(name="spread", bufs=3))
         stack.enter_context(tc.manual_schedule())
 
         one = keep.tile([P, 1], F32)
@@ -61,21 +64,36 @@ def tile_pnn_v_kernel(tc, x, centers, probs, grad_out, out):
 
         prob = {}
         grad = {}
-        pair_sums = {}
         centre = {}
         weight = {}
-        factors = {}
-        codes = {}
-        sums = {}
+        group = {}
+        grouped = {}
+        w_codes = {}
+        w_scales = {}
+        minus_sum = {}
+        acc = {}
         x_tiles = {}
+
+        def rows_of_pass(dram, c):
+            return dram[c * K_PASS : (c + 1) * K_PASS]
 
         def load_prob(i):
             prob[i] = prob_pool.tile([P, PASSES, PACK, COLS], F32, name="prob")
             for c in range(PASSES):
                 nc.sync.dma_start(
                     out=prob[i][:, c],
-                    in_=probs[c * K_PASS : (c + 1) * K_PASS, i * O_CHUNK : (i + 1) * O_CHUNK, :].rearrange(
+                    in_=rows_of_pass(probs, c)[:, i * O_CHUNK : (i + 1) * O_CHUNK, :].rearrange(
                         "(p j) o m -> p j (o m)", j=PACK
+                    ),
+                )
+
+        def load_grad(i):
+            grad[i] = stream.tile([P, ROWS, O_CHUNK], BF16, name="grad")
+            for c in range(PASSES):
+                nc.sync.dma_start(
+                    out=grad[i][:, c * PACK : (c + 1) * PACK, :],
+                    in_=rows_of_pass(grad_out, c)[:, i * O_CHUNK : (i + 1) * O_CHUNK].rearrange(
+                        "(p j) o -> p j o", j=PACK
                     ),
                 )
 
@@ -86,25 +104,12 @@ def tile_pnn_v_kernel(tc, x, centers, probs, grad_out, out):
                 in_=centre_rows[i * COLS : (i + 1) * COLS, :].rearrange("(t p) d -> p t d", p=P),
             )
 
-        def load_grad(i):
-            grad[i] = stream.tile([P, ROWS, O_CHUNK], BF16, name="grad")
-            for c in range(PASSES):
-                nc.sync.dma_start(
-                    out=grad[i][:, c * PACK : (c + 1) * PACK, :],
-                    in_=grad_out[c * K_PASS : (c + 1) * K_PASS, i * O_CHUNK : (i + 1) * O_CHUNK].rearrange(
-                        "(p j) o -> p j o", j=PACK
-                    ),
-                )
-
         def load_x(c):
-            x_raw = xstage.tile([P, PACK, D], BF16, name="x_raw")
-            nc.sync.dma_start(
-                out=x_raw[:], in_=x[c * K_PASS : (c + 1) * K_PASS, :].rearrange("(p j) d -> p j d", j=PACK)
-            )
-            x_tiles[c] = x_raw
+            x_tiles[c] = x_stage.tile([P, PACK, D], BF16, name="x_raw")
+            nc.sync.dma_start(out=x_tiles[c][:], in_=rows_of_pass(x, c).rearrange("(p j) d -> p j d", j=PACK))
 
         def regroup_x(c):
-            x_grouped = xstage.tile([P, D, PACK], BF16, align_bytes=64, name="x_grouped")
+            x_grouped = x_stage.tile([P, D, PACK], BF16, align_bytes=64, name="x_grouped")
             nc.scalar.copy(out=x_grouped[:], in_=x_tiles[c][:].rearrange("p j d -> p d j"))
             x_tiles[c] = x_grouped
 
@@ -115,182 +120,177 @@ def tile_pnn_v_kernel(tc, x, centers, probs, grad_out, out):
                 in_=x_tiles[c][:].rearrange("p d j -> p (d j)"),
             )
 
-        def by_group(tile_ap):
-            return tile_ap.rearrange("p c j (o m) -> p (c j o) m", m=M)
-
-        def sum_pairs(i):
-            prob4 = by_group(prob[i][:])
-            pair_sums[i] = small.tile([P, GROUPS, 2], F32, name="pair_sum")
-            nc.gpsimd.tensor_tensor(out=pair_sums[i][:], in0=prob4[:, :, 0:2], in1=prob4[:, :, 2:4], op=ALU.add)
-
-        def front(i):
-            prob4 = by_group(prob[i][:])
-            pair_sum = pair_sums[i]
-            pair_max = small.tile([P, GROUPS, 2], F32, name="pair_max")
-            top = small.tile([P, GROUPS, 1], F32, name="top")
-            total = small.tile([P, GROUPS, 1], F32, name="total")
-            den = small.tile([P, GROUPS, 1], F32, name="den", tag="den_then_corr")
-            nc.vector.tensor_tensor(out=pair_max[:], in0=prob4[:, :, 0:2], in1=prob4[:, :, 2:4], op=ALU.max)
-            nc.vector.tensor_tensor(out=top[:], in0=pair_max[:, :, 0:1], in1=pair_max[:, :, 1:2], op=ALU.max)
-            nc.vector.tensor_tensor(out=total[:], in0=pair_sum[:, :, 0:1], in1=pair_sum[:, :, 1:2], op=ALU.add)
-            nc.vector.scalar_tensor_tensor(
-                out=den[:], in0=top[:], scalar=-4.0, in1=total[:], op0=ALU.mult, op1=ALU.add
-            )
-            dsq = small.tile([P, GROUPS, 1], F32, name="dsq")
-            seed = small.tile([P, GROUPS, 1], F32, name="seed")
-            rest = small.tile([P, GROUPS, 1], F32, name="rest")
-            nc.scalar.activation(out=dsq[:], in_=den[:], func=ACT.Square, bias=one[:, 0:1], scale=0.25)
-            nc.scalar.activation(out=seed[:], in_=dsq[:], func=ACT.Square)
-            nc.scalar.activation(out=seed[:], in_=seed[:], func=ACT.Abs_reciprocal_sqrt)
-            nc.scalar.activation(out=rest[:], in_=top[:], func=ACT.Identity, bias=minus_one[:, 0:1], scale=1.0)
-            factors[i] = {"top": top, "total": total, "dsq": dsq, "seed": seed, "rest": rest}
+        def by_group(chunk_tile):
+            return chunk_tile[:].rearrange("p c j (o m) -> p (c j o) m", m=M)
 
         def half(h):
             return slice(h * HALF, (h + 1) * HALF)
 
-        def spread(values, h):
-            bank = spread_pool.tile([P, HALF, 1], F32, name="bank")
-            nc.tensor.matmul(out=bank[:, :, 0], lhsT=ident[:], rhs=values[:, half(h), 0], start=True, stop=True)
+        def passes_of_half(h):
+            return slice(h * HALF_PASSES, (h + 1) * HALF_PASSES)
+
+        def per_group(name):
+            return small.tile([P, GROUPS, 1], F32, name=name)
+
+        def pair_up(i):
+            g = {"pair_max": small.tile([P, GROUPS, 2], F32, name="pair_max")}
+            g["pair_sum"] = small.tile([P, GROUPS, 2], F32, name="pair_sum")
+            group[i] = g
+            components = by_group(prob[i])
+            nc.vector.tensor_tensor(out=g["pair_max"][:], in0=components[:, :, 0:2], in1=components[:, :, 2:4], op=ALU.max)
+            nc.vector.tensor_tensor(out=g["pair_sum"][:], in0=components[:, :, 0:2], in1=components[:, :, 2:4], op=ALU.add)
+
+        def reduce_pairs(i):
+            g = group[i]
+            g["top"] = per_group("top")
+            g["total"] = per_group("total")
+            nc.vector.tensor_tensor(
+                out=g["top"][:], in0=g["pair_max"][:, :, 0:1], in1=g["pair_max"][:, :, 1:2], op=ALU.max
+            )
+            nc.vector.tensor_tensor(
+                out=g["total"][:], in0=g["pair_sum"][:, :, 0:1], in1=g["pair_sum"][:, :, 1:2], op=ALU.add
+            )
+
+        def denominator(i):
+            g = group[i]
+            den_minus_4 = per_group("den_minus_4")
+            g["den_sq_16"] = per_group("den_sq_16")
+            g["seed"] = per_group("seed")
+            g["minus_rest"] = per_group("minus_rest")
+            nc.vector.scalar_tensor_tensor(
+                out=den_minus_4[:], in0=g["top"][:], scalar=-4.0, in1=g["total"][:], op0=ALU.mult, op1=ALU.add
+            )
+            nc.scalar.activation(out=g["den_sq_16"][:], in_=den_minus_4[:], func=ACT.Square, bias=one[:, 0:1], scale=0.25)
+            nc.scalar.activation(out=g["seed"][:], in_=g["den_sq_16"][:], func=ACT.Square)
+            nc.scalar.activation(out=g["seed"][:], in_=g["seed"][:], func=ACT.Abs_reciprocal_sqrt)
+            nc.scalar.activation(
+                out=g["minus_rest"][:], in_=g["top"][:], func=ACT.Identity, bias=minus_one[:, 0:1], scale=1.0
+            )
+
+        def start_gain(i):
+            g = group[i]
+            g["seed_grad"] = per_group("seed_grad")
+            g["near_one"] = per_group("near_one")
+            by_row = "p (r o) u -> p r (o u)"
+            nc.vector.tensor_tensor(
+                out=g["seed_grad"][:].rearrange(by_row, o=O_CHUNK),
+                in0=g["seed"][:].rearrange(by_row, o=O_CHUNK),
+                in1=grad[i][:],
+                op=ALU.mult,
+            )
+            nc.vector.tensor_tensor(out=g["near_one"][:], in0=g["den_sq_16"][:], in1=g["seed"][:], op=ALU.mult)
+
+        def finish_gain(i):
+            g = group[i]
+            g["minus_gain"] = per_group("minus_gain")
+            nc.vector.scalar_tensor_tensor(
+                out=g["minus_gain"][:],
+                in0=g["near_one"][:],
+                scalar=2.0,
+                in1=g["seed_grad"][:],
+                op0=ALU.subtract,
+                op1=ALU.mult,
+            )
+
+        def make_base(i):
+            g = group[i]
+            g["base"] = per_group("base")
+            nc.vector.tensor_tensor(out=g["base"][:], in0=g["minus_rest"][:], in1=g["minus_gain"][:], op=ALU.mult)
+
+        def make_bonus(i):
+            g = group[i]
+            g["bonus"] = per_group("bonus")
+            nc.vector.scalar_tensor_tensor(
+                out=g["bonus"][:], in0=g["total"][:], scalar=-1.0, in1=g["minus_gain"][:], op0=ALU.mult, op1=ALU.mult
+            )
+
+        def copy_to_psum(i, name, h):
+            bank = copy_pool.tile([P, HALF, 1], F32, name="bank")
+            nc.tensor.matmul(out=bank[:, :, 0], lhsT=ident[:], rhs=group[i][name][:, half(h), 0], start=True, stop=True)
             return bank
 
-        def with_factor(i, h, bank, op, source):
+        def combine(i, h, source, op, bank):
             nc.vector.tensor_tensor(
-                out=by_group(weight[i][:])[:, half(h), :],
-                in0=by_group(source[i][:])[:, half(h), :],
+                out=by_group(weight[i])[:, half(h), :],
+                in0=by_group(source[i])[:, half(h), :],
                 in1=bank[:].to_broadcast([P, HALF, M]),
                 op=op,
             )
 
-        def mark_top(i, banks):
-            weight[i] = stream.tile([P, PASSES, PACK, COLS], F32, name="weight")
-            for h in range(HALVES):
-                with_factor(i, h, banks[h], ALU.is_equal, prob)
+        def times_prob(engine, i, h):
+            cs = passes_of_half(h)
+            engine.tensor_tensor(out=weight[i][:, cs], in0=weight[i][:, cs], in1=prob[i][:, cs], op=ALU.mult)
 
-        def make_factors(i):
-            f = factors[i]
-            corr = small.tile([P, GROUPS, 1], F32, name="corr", tag="den_then_corr")
-            gain = small.tile([P, GROUPS, 1], F32, name="gain")
-            base = small.tile([P, GROUPS, 1], F32, name="base")
-            bonus = small.tile([P, GROUPS, 1], F32, name="bonus")
-            nc.vector.tensor_tensor(
-                out=gain[:].rearrange("p (r o) u -> p r (o u)", o=O_CHUNK),
-                in0=f["seed"][:].rearrange("p (r o) u -> p r (o u)", o=O_CHUNK),
-                in1=grad[i][:],
-                op=ALU.mult,
-            )
-            nc.vector.tensor_tensor(out=corr[:], in0=f["dsq"][:], in1=f["seed"][:], op=ALU.mult)
-            nc.vector.scalar_tensor_tensor(
-                out=gain[:], in0=corr[:], scalar=2.0, in1=gain[:], op0=ALU.subtract, op1=ALU.mult
-            )
-            nc.vector.tensor_tensor(out=base[:], in0=f["rest"][:], in1=gain[:], op=ALU.mult)
-            nc.vector.scalar_tensor_tensor(
-                out=bonus[:], in0=f["total"][:], scalar=-1.0, in1=gain[:], op0=ALU.mult, op1=ALU.mult
-            )
-            f["base"] = base
-            f["bonus"] = bonus
-
-        def first_spreads(i):
-            f = factors[i]
-            return [spread(f["bonus"], 0), spread(f["base"], 0), spread(f["bonus"], 1)]
-
-        def last_factor(i, h):
-            nc.gpsimd.tensor_tensor(
-                out=by_group(weight[i][:])[:, half(h), :],
-                in0=by_group(weight[i][:])[:, half(h), :],
-                in1=by_group(prob[i][:])[:, half(h), :],
-                op=ALU.mult,
-            )
-
-        def make_weights(i, banks):
-            bonus_0, base_0, bonus_1 = banks
-            tops = []
-            with_factor(i, 0, bonus_0, ALU.mult, weight)
-            base_1 = spread(factors[i]["base"], 1)
-            with_factor(i, 0, base_0, ALU.add, weight)
-            last_factor(i, 0)
-            if i + 1 < CHUNKS:
-                tops.append(spread(factors[i + 1]["top"], 0))
-            with_factor(i, 1, bonus_1, ALU.mult, weight)
-            if i + 1 < CHUNKS:
-                tops.append(spread(factors[i + 1]["top"], 1))
-            with_factor(i, 1, base_1, ALU.add, weight)
-            last_factor(i, 1)
-            return tops
-
-        def regroup(i):
-            grouped = quant.tile([P, PASSES, COLS, PACK], BF16, align_bytes=64, name="grouped")
-            per_half = PASSES // HALVES
-            for h in range(HALVES):
-                cs = slice(h * per_half, (h + 1) * per_half)
-                nc.scalar.copy(out=grouped[:, cs], in_=weight[i][:, cs].rearrange("p c j w -> p c w j"))
-            codes[i] = {"grouped": grouped}
+        def regroup(i, h):
+            if h == 0:
+                grouped[i] = quant.tile([P, PASSES, COLS, PACK], BF16, align_bytes=64, name="grouped")
+            cs = passes_of_half(h)
+            nc.scalar.copy(out=grouped[i][:, cs], in_=weight[i][:, cs].rearrange("p c j w -> p c w j"))
 
         def column_sums(i):
-            minus_sum_ps = sum_pool.tile([P, M_TILES], F32, name="minus_sum_ps")
-            sums[i] = minus_sum_ps
+            minus_sum[i] = sum_pool.tile([P, M_TILES], F32, name="minus_sum_psum")
             for t in range(M_TILES):
                 for r in range(ROWS):
                     nc.tensor.matmul(
-                        out=minus_sum_ps[:, t : t + 1],
+                        out=minus_sum[i][:, t : t + 1],
                         lhsT=weight[i][:, r // PACK, r % PACK, t * M_TILE : (t + 1) * M_TILE],
                         rhs=minus_one[:],
                         start=(r == 0),
                         stop=(r == ROWS - 1),
                     )
 
-        def quantise(i):
-            w_codes = quant.tile([P, PASSES * COLS], U32, align_bytes=64, name="w_codes")
-            w_scales = quant.tile([P, PASSES * COLS], U8, align_bytes=64, name="w_scales")
-            words = PASSES * COLS // HALVES
-            per_half = PASSES // HALVES
-            for h in range(HALVES):
-                nc.vector.quantize_mx(
-                    out=w_codes[:, h * words : (h + 1) * words].bitcast(E5M2X4),
-                    scales=w_scales[:, h * words : (h + 1) * words],
-                    in_=codes[i]["grouped"][:, h * per_half : (h + 1) * per_half].rearrange("p c w j -> p (c w j)"),
-                )
-            codes[i]["w_codes"] = w_codes
-            codes[i]["w_scales"] = w_scales
+        def quantise(i, h):
+            if h == 0:
+                w_codes[i] = quant.tile([P, PASSES * COLS], U32, align_bytes=64, name="w_codes")
+                w_scales[i] = quant.tile([P, PASSES * COLS], U8, align_bytes=64, name="w_scales")
+            words = slice(h * HALF_WORDS, (h + 1) * HALF_WORDS)
+            nc.vector.quantize_mx(
+                out=w_codes[i][:, words].bitcast(E5M2X4),
+                scales=w_scales[i][:, words],
+                in_=grouped[i][:, passes_of_half(h)].rearrange("p c w j -> p (c w j)"),
+            )
 
         def products(i):
-            w_codes = codes[i]["w_codes"]
-            w_scales = codes[i]["w_scales"]
-            minus_sum = result.tile([P, M_TILES], F32, name="minus_sum")
-            nc.scalar.copy(out=minus_sum[:], in_=sums[i][:])
-            sums[i] = minus_sum
-            accs = [acc_pool.tile([P, N_TILE], F32, name="acc") for k in range(M_TILES * N_TILES)]
+            in_sbuf = result.tile([P, M_TILES], F32, name="minus_sum")
+            nc.scalar.copy(out=in_sbuf[:], in_=minus_sum[i][:])
+            minus_sum[i] = in_sbuf
+            acc[i] = [acc_pool.tile([P, N_TILE], F32, name="acc") for k in range(OUT_TILES)]
             for c in range(PASSES):
-                for t in range(M_TILES):
-                    for n in range(N_TILES):
-                        w_cols = slice(c * COLS + t * M_TILE, c * COLS + (t + 1) * M_TILE)
-                        x_cols = slice(n * N_TILE, (n + 1) * N_TILE)
-                        nc.tensor.matmul_mx(
-                            out=accs[t * N_TILES + n][:],
-                            lhsT=w_codes[:, w_cols].bitcast(E5M2X4),
-                            lhsT_scale=w_scales[:, w_cols],
-                            rhs=x_codes[:, c, x_cols].bitcast(E4M3X4),
-                            rhs_scale=x_scales[:, c, x_cols],
-                            start=(c == 0),
-                            stop=(c == PASSES - 1),
-                        )
-            codes[i]["accs"] = accs
+                for k in range(OUT_TILES):
+                    t, n = k // N_TILES, k % N_TILES
+                    w_cols = slice(c * COLS + t * M_TILE, c * COLS + (t + 1) * M_TILE)
+                    x_cols = slice(n * N_TILE, (n + 1) * N_TILE)
+                    nc.tensor.matmul_mx(
+                        out=acc[i][k][:],
+                        lhsT=w_codes[i][:, w_cols].bitcast(E5M2X4),
+                        lhsT_scale=w_scales[i][:, w_cols],
+                        rhs=x_codes[:, c, x_cols].bitcast(E4M3X4),
+                        rhs_scale=x_scales[:, c, x_cols],
+                        start=(c == 0),
+                        stop=(c == PASSES - 1),
+                    )
 
-        def finish(i):
-            for t in range(M_TILES):
-                for n in range(N_TILES):
-                    res = result.tile([P, N_TILE], F32, name="res")
-                    nc.vector.scalar_tensor_tensor(
-                        out=res[:],
-                        in0=centre[i][:, t, n * N_TILE : (n + 1) * N_TILE],
-                        scalar=sums[i][:, t : t + 1],
-                        in1=codes[i]["accs"][t * N_TILES + n][:],
-                        op0=ALU.mult,
-                        op1=ALU.add,
-                    )
-                    row0 = i * COLS + t * M_TILE
-                    nc.sync.dma_start(
-                        out=out_rows[row0 : row0 + M_TILE, n * N_TILE : (n + 1) * N_TILE], in_=res[:]
-                    )
+        def finish(i, k):
+            if i < 0:
+                return
+            t, n = k // N_TILES, k % N_TILES
+            d_cols = slice(n * N_TILE, (n + 1) * N_TILE)
+            res = result.tile([P, N_TILE], F32, name="res")
+            nc.vector.scalar_tensor_tensor(
+                out=res[:],
+                in0=centre[i][:, t, d_cols],
+                scalar=minus_sum[i][:, t : t + 1],
+                in1=acc[i][k][:],
+                op0=ALU.mult,
+                op1=ALU.add,
+            )
+            row0 = i * COLS + t * M_TILE
+            nc.sync.dma_start(out=out_rows[row0 : row0 + M_TILE, d_cols], in_=res[:])
+
+        def mark_top(i, banks):
+            weight[i] = stream.tile([P, PASSES, PACK, COLS], F32, name="weight")
+            for h in range(HALVES):
+                combine(i, h, prob, ALU.is_equal, banks[h])
 
         load_prob(0)
         load_grad(0)
@@ -299,44 +299,82 @@ def tile_pnn_v_kernel(tc, x, centers, probs, grad_out, out):
         load_prob(1)
         load_grad(1)
         load_centre(0)
-        sum_pairs(0)
-        front(0)
-        sum_pairs(1)
-        mark_top(0, [spread(factors[0]["top"], 0), spread(factors[0]["top"], 1)])
+        pair_up(0)
+        reduce_pairs(0)
+        denominator(0)
+        mark_top(0, [copy_to_psum(0, "top", h) for h in range(HALVES)])
         regroup_x(0)
         regroup_x(1)
         load_x(2)
         load_x(3)
         load_prob(2)
-        make_factors(0)
-        banks = first_spreads(0)
-        for i in range(CHUNKS):
-            if i + 1 < CHUNKS:
-                front(i + 1)
+        start_gain(0)
+        finish_gain(0)
+        make_base(0)
+        make_bonus(0)
+        bonus_0, base_0, bonus_1 = copy_to_psum(0, "bonus", 0), copy_to_psum(0, "base", 0), copy_to_psum(0, "bonus", 1)
+
+        for i in range(CHUNKS - 1):
+            pair_up(i + 1)
+            reduce_pairs(i + 1)
             if i + 2 < CHUNKS:
-                sum_pairs(i + 2)
                 load_grad(i + 2)
+            combine(i, 0, weight, ALU.mult, bonus_0)
+            base_1 = copy_to_psum(i, "base", 1)
+            denominator(i + 1)
             if i == 0:
                 quantise_x(0)
                 quantise_x(1)
                 regroup_x(2)
                 regroup_x(3)
-            tops = make_weights(i, banks)
+            combine(i, 0, weight, ALU.add, base_0)
+            times_prob(nc.gpsimd, i, 0)
+            top_0 = copy_to_psum(i + 1, "top", 0)
+            combine(i, 1, weight, ALU.mult, bonus_1)
+            top_1 = copy_to_psum(i + 1, "top", 1)
+            finish(i - 1, 0)
+            combine(i, 1, weight, ALU.add, base_1)
+            times_prob(nc.gpsimd, i, 1)
             if i + 3 < CHUNKS:
                 load_prob(i + 3)
-            regroup(i)
+            regroup(i, 0)
+            regroup(i, 1)
             column_sums(i)
-            if i + 1 < CHUNKS:
-                mark_top(i + 1, tops)
-            if i >= 1:
-                finish(i - 1)
-            if i + 1 < CHUNKS:
-                load_centre(i + 1)
-                make_factors(i + 1)
-                banks = first_spreads(i + 1)
+            mark_top(i + 1, [top_0, top_1])
+            finish(i - 1, 1)
+            finish(i - 1, 2)
+            start_gain(i + 1)
+            finish(i - 1, 3)
+            load_centre(i + 1)
+            finish_gain(i + 1)
             if i == 0:
                 quantise_x(2)
                 quantise_x(3)
-            quantise(i)
+            quantise(i, 0)
+            make_base(i + 1)
+            make_bonus(i + 1)
+            bonus_0, base_0, bonus_1 = (
+                copy_to_psum(i + 1, "bonus", 0),
+                copy_to_psum(i + 1, "base", 0),
+                copy_to_psum(i + 1, "bonus", 1),
+            )
+            quantise(i, 1)
             products(i)
-        finish(CHUNKS - 1)
+
+        last = CHUNKS - 1
+        combine(last, 0, weight, ALU.mult, bonus_0)
+        base_1 = copy_to_psum(last, "base", 1)
+        combine(last, 1, weight, ALU.mult, bonus_1)
+        combine(last, 0, weight, ALU.add, base_0)
+        combine(last, 1, weight, ALU.add, base_1)
+        for h in range(HALVES):
+            times_prob(nc.vector, last, h)
+            regroup(last, h)
+        column_sums(last)
+        for k in range(OUT_TILES):
+            finish(last - 1, k)
+        for h in range(HALVES):
+            quantise(last, h)
+        products(last)
+        for k in range(OUT_TILES):
+            finish(last, k)

from contextlib import ExitStack

import concourse.mybir as mybir
from concourse.masks import make_identity

F32 = mybir.dt.float32
BF16 = mybir.dt.bfloat16
U32 = mybir.dt.uint32
U8 = mybir.dt.uint8
E4M3X4 = mybir.dt.float8_e4m3fn_x4
E5M2X4 = mybir.dt.float8_e5m2_x4
ALU = mybir.AluOpType
ACT = mybir.ActivationFunctionType

B, D, O, M = 2048, 1024, 512, 4
P = 128
PACK = 4
K_PASS = P * PACK
PASSES = B // K_PASS
ROWS = PASSES * PACK
O_CHUNK = 64
COLS = O_CHUNK * M
CHUNKS = O // O_CHUNK
GROUPS = ROWS * O_CHUNK
HALVES = 2
HALF = GROUPS // HALVES
HALF_PASSES = PASSES // HALVES
HALF_WORDS = HALF_PASSES * COLS
M_TILE = 128
M_TILES = COLS // M_TILE
N_TILE = 512
N_TILES = D // N_TILE
OUT_TILES = M_TILES * N_TILES

FLOPS = 2 * B * O * M * D


def tile_pnn_v_kernel(tc, x, centers, probs, grad_out, out):
    nc = tc.nc
    centre_rows = centers.rearrange("o m d -> (o m) d")
    out_rows = out.rearrange("o m d -> (o m) d")

    with ExitStack() as stack:
        keep = stack.enter_context(tc.tile_pool(name="keep", bufs=1))
        x_stage = stack.enter_context(tc.tile_pool(name="x_stage", bufs=2))
        prob_pool = stack.enter_context(tc.tile_pool(name="prob_pool", bufs=3))
        stream = stack.enter_context(tc.tile_pool(name="stream", bufs=2))
        small = stack.enter_context(tc.tile_pool(name="small", bufs=1))
        quant = stack.enter_context(tc.tile_pool(name="quant", bufs=2))
        result = stack.enter_context(tc.tile_pool(name="result", bufs=OUT_TILES))
        acc_pool = stack.enter_context(tc.psum_pool(name="acc", bufs=OUT_TILES))
        copy_pool = stack.enter_context(tc.psum_pool(name="copies", bufs=3))
        sum_pool = stack.enter_context(tc.psum_pool(name="sums", bufs=1))
        stack.enter_context(tc.manual_schedule())

        one = keep.tile([P, 1], F32)
        nc.vector.memset(one[:], 1.0)
        minus_one = keep.tile([P, 1], F32)
        nc.vector.memset(minus_one[:], -1.0)
        ident = keep.tile([P, P], F32)
        make_identity(nc, ident[:])
        x_codes = keep.tile([P, PASSES, D], U32, align_bytes=64)
        x_scales = keep.tile([P, PASSES, D], U8, align_bytes=64)

        prob = {}
        grad = {}
        centre = {}
        weight = {}
        group = {}
        grouped = {}
        w_codes = {}
        w_scales = {}
        minus_sum = {}
        acc = {}
        x_tiles = {}

        def rows_of_pass(dram, c):
            return dram[c * K_PASS : (c + 1) * K_PASS]

        def load_prob(i):
            prob[i] = prob_pool.tile([P, PASSES, PACK, COLS], F32, name="prob")
            for c in range(PASSES):
                nc.sync.dma_start(
                    out=prob[i][:, c],
                    in_=rows_of_pass(probs, c)[:, i * O_CHUNK : (i + 1) * O_CHUNK, :].rearrange(
                        "(p j) o m -> p j (o m)", j=PACK
                    ),
                )

        def load_grad(i):
            grad[i] = stream.tile([P, ROWS, O_CHUNK], BF16, name="grad")
            for c in range(PASSES):
                nc.sync.dma_start(
                    out=grad[i][:, c * PACK : (c + 1) * PACK, :],
                    in_=rows_of_pass(grad_out, c)[:, i * O_CHUNK : (i + 1) * O_CHUNK].rearrange(
                        "(p j) o -> p j o", j=PACK
                    ),
                )

        def load_centre(i):
            centre[i] = stream.tile([P, M_TILES, D], BF16, name="centre")
            nc.sync.dma_start(
                out=centre[i][:],
                in_=centre_rows[i * COLS : (i + 1) * COLS, :].rearrange("(t p) d -> p t d", p=P),
            )

        def load_x(c):
            x_tiles[c] = x_stage.tile([P, PACK, D], BF16, name="x_raw")
            nc.sync.dma_start(out=x_tiles[c][:], in_=rows_of_pass(x, c).rearrange("(p j) d -> p j d", j=PACK))

        def regroup_x(c):
            x_grouped = x_stage.tile([P, D, PACK], BF16, align_bytes=64, name="x_grouped")
            nc.scalar.copy(out=x_grouped[:], in_=x_tiles[c][:].rearrange("p j d -> p d j"))
            x_tiles[c] = x_grouped

        def quantise_x(c):
            nc.vector.quantize_mx(
                out=x_codes[:, c, :].bitcast(E4M3X4),
                scales=x_scales[:, c, :],
                in_=x_tiles[c][:].rearrange("p d j -> p (d j)"),
            )

        def by_group(chunk_tile):
            return chunk_tile[:].rearrange("p c j (o m) -> p (c j o) m", m=M)

        def half(h):
            return slice(h * HALF, (h + 1) * HALF)

        def passes_of_half(h):
            return slice(h * HALF_PASSES, (h + 1) * HALF_PASSES)

        def per_group(name):
            return small.tile([P, GROUPS, 1], F32, name=name)

        def pair_up(i):
            g = {"pair_max": small.tile([P, GROUPS, 2], F32, name="pair_max")}
            g["pair_sum"] = small.tile([P, GROUPS, 2], F32, name="pair_sum")
            group[i] = g
            components = by_group(prob[i])
            nc.vector.tensor_tensor(out=g["pair_max"][:], in0=components[:, :, 0:2], in1=components[:, :, 2:4], op=ALU.max)
            nc.vector.tensor_tensor(out=g["pair_sum"][:], in0=components[:, :, 0:2], in1=components[:, :, 2:4], op=ALU.add)

        def reduce_pairs(i):
            g = group[i]
            g["top"] = per_group("top")
            g["total"] = per_group("total")
            nc.vector.tensor_tensor(
                out=g["top"][:], in0=g["pair_max"][:, :, 0:1], in1=g["pair_max"][:, :, 1:2], op=ALU.max
            )
            nc.vector.tensor_tensor(
                out=g["total"][:], in0=g["pair_sum"][:, :, 0:1], in1=g["pair_sum"][:, :, 1:2], op=ALU.add
            )

        def denominator(i):
            g = group[i]
            den_minus_4 = per_group("den_minus_4")
            g["den_sq_16"] = per_group("den_sq_16")
            g["seed"] = per_group("seed")
            g["minus_rest"] = per_group("minus_rest")
            nc.vector.scalar_tensor_tensor(
                out=den_minus_4[:], in0=g["top"][:], scalar=-4.0, in1=g["total"][:], op0=ALU.mult, op1=ALU.add
            )
            nc.scalar.activation(out=g["den_sq_16"][:], in_=den_minus_4[:], func=ACT.Square, bias=one[:, 0:1], scale=0.25)
            nc.scalar.activation(out=g["seed"][:], in_=g["den_sq_16"][:], func=ACT.Square)
            nc.scalar.activation(out=g["seed"][:], in_=g["seed"][:], func=ACT.Abs_reciprocal_sqrt)
            nc.scalar.activation(
                out=g["minus_rest"][:], in_=g["top"][:], func=ACT.Identity, bias=minus_one[:, 0:1], scale=1.0
            )

        def start_gain(i):
            g = group[i]
            g["seed_grad"] = per_group("seed_grad")
            g["near_one"] = per_group("near_one")
            by_row = "p (r o) u -> p r (o u)"
            nc.vector.tensor_tensor(
                out=g["seed_grad"][:].rearrange(by_row, o=O_CHUNK),
                in0=g["seed"][:].rearrange(by_row, o=O_CHUNK),
                in1=grad[i][:],
                op=ALU.mult,
            )
            nc.vector.tensor_tensor(out=g["near_one"][:], in0=g["den_sq_16"][:], in1=g["seed"][:], op=ALU.mult)

        def finish_gain(i):
            g = group[i]
            g["minus_gain"] = per_group("minus_gain")
            nc.vector.scalar_tensor_tensor(
                out=g["minus_gain"][:],
                in0=g["near_one"][:],
                scalar=2.0,
                in1=g["seed_grad"][:],
                op0=ALU.subtract,
                op1=ALU.mult,
            )

        def make_base(i):
            g = group[i]
            g["base"] = per_group("base")
            nc.vector.tensor_tensor(out=g["base"][:], in0=g["minus_rest"][:], in1=g["minus_gain"][:], op=ALU.mult)

        def make_bonus(i):
            g = group[i]
            g["bonus"] = per_group("bonus")
            nc.vector.scalar_tensor_tensor(
                out=g["bonus"][:], in0=g["total"][:], scalar=-1.0, in1=g["minus_gain"][:], op0=ALU.mult, op1=ALU.mult
            )

        def copy_to_psum(i, name, h):
            bank = copy_pool.tile([P, HALF, 1], F32, name="bank")
            nc.tensor.matmul(out=bank[:, :, 0], lhsT=ident[:], rhs=group[i][name][:, half(h), 0], start=True, stop=True)
            return bank

        def combine(i, h, source, op, bank):
            nc.vector.tensor_tensor(
                out=by_group(weight[i])[:, half(h), :],
                in0=by_group(source[i])[:, half(h), :],
                in1=bank[:].to_broadcast([P, HALF, M]),
                op=op,
            )

        def times_prob(engine, i, h):
            cs = passes_of_half(h)
            engine.tensor_tensor(out=weight[i][:, cs], in0=weight[i][:, cs], in1=prob[i][:, cs], op=ALU.mult)

        def regroup(i, h):
            if h == 0:
                grouped[i] = quant.tile([P, PASSES, COLS, PACK], BF16, align_bytes=64, name="grouped")
            cs = passes_of_half(h)
            nc.scalar.copy(out=grouped[i][:, cs], in_=weight[i][:, cs].rearrange("p c j w -> p c w j"))

        def column_sums(i):
            minus_sum[i] = sum_pool.tile([P, M_TILES], F32, name="minus_sum_psum")
            for t in range(M_TILES):
                for r in range(ROWS):
                    nc.tensor.matmul(
                        out=minus_sum[i][:, t : t + 1],
                        lhsT=weight[i][:, r // PACK, r % PACK, t * M_TILE : (t + 1) * M_TILE],
                        rhs=minus_one[:],
                        start=(r == 0),
                        stop=(r == ROWS - 1),
                    )

        def quantise(i, h):
            if h == 0:
                w_codes[i] = quant.tile([P, PASSES * COLS], U32, align_bytes=64, name="w_codes")
                w_scales[i] = quant.tile([P, PASSES * COLS], U8, align_bytes=64, name="w_scales")
            words = slice(h * HALF_WORDS, (h + 1) * HALF_WORDS)
            nc.vector.quantize_mx(
                out=w_codes[i][:, words].bitcast(E5M2X4),
                scales=w_scales[i][:, words],
                in_=grouped[i][:, passes_of_half(h)].rearrange("p c w j -> p (c w j)"),
            )

        def products(i):
            in_sbuf = result.tile([P, M_TILES], F32, name="minus_sum")
            nc.scalar.copy(out=in_sbuf[:], in_=minus_sum[i][:])
            minus_sum[i] = in_sbuf
            acc[i] = [acc_pool.tile([P, N_TILE], F32, name="acc") for k in range(OUT_TILES)]
            for c in range(PASSES):
                for k in range(OUT_TILES):
                    t, n = k // N_TILES, k % N_TILES
                    w_cols = slice(c * COLS + t * M_TILE, c * COLS + (t + 1) * M_TILE)
                    x_cols = slice(n * N_TILE, (n + 1) * N_TILE)
                    nc.tensor.matmul_mx(
                        out=acc[i][k][:],
                        lhsT=w_codes[i][:, w_cols].bitcast(E5M2X4),
                        lhsT_scale=w_scales[i][:, w_cols],
                        rhs=x_codes[:, c, x_cols].bitcast(E4M3X4),
                        rhs_scale=x_scales[:, c, x_cols],
                        start=(c == 0),
                        stop=(c == PASSES - 1),
                    )

        def finish(i, k):
            if i < 0:
                return
            t, n = k // N_TILES, k % N_TILES
            d_cols = slice(n * N_TILE, (n + 1) * N_TILE)
            res = result.tile([P, N_TILE], F32, name="res")
            nc.vector.scalar_tensor_tensor(
                out=res[:],
                in0=centre[i][:, t, d_cols],
                scalar=minus_sum[i][:, t : t + 1],
                in1=acc[i][k][:],
                op0=ALU.mult,
                op1=ALU.add,
            )
            row0 = i * COLS + t * M_TILE
            nc.sync.dma_start(out=out_rows[row0 : row0 + M_TILE, d_cols], in_=res[:])

        def mark_top(i, banks):
            weight[i] = stream.tile([P, PASSES, PACK, COLS], F32, name="weight")
            for h in range(HALVES):
                combine(i, h, prob, ALU.is_equal, banks[h])

        load_prob(0)
        load_grad(0)
        load_x(0)
        load_x(1)
        load_prob(1)
        load_grad(1)
        load_centre(0)
        pair_up(0)
        reduce_pairs(0)
        denominator(0)
        mark_top(0, [copy_to_psum(0, "top", h) for h in range(HALVES)])
        regroup_x(0)
        regroup_x(1)
        load_x(2)
        load_x(3)
        load_prob(2)
        start_gain(0)
        finish_gain(0)
        make_base(0)
        make_bonus(0)
        bonus_0, base_0, bonus_1 = copy_to_psum(0, "bonus", 0), copy_to_psum(0, "base", 0), copy_to_psum(0, "bonus", 1)

        for i in range(CHUNKS - 1):
            pair_up(i + 1)
            reduce_pairs(i + 1)
            if i + 2 < CHUNKS:
                load_grad(i + 2)
            combine(i, 0, weight, ALU.mult, bonus_0)
            base_1 = copy_to_psum(i, "base", 1)
            denominator(i + 1)
            if i == 0:
                quantise_x(0)
                quantise_x(1)
                regroup_x(2)
                regroup_x(3)
            combine(i, 0, weight, ALU.add, base_0)
            times_prob(nc.gpsimd, i, 0)
            top_0 = copy_to_psum(i + 1, "top", 0)
            combine(i, 1, weight, ALU.mult, bonus_1)
            top_1 = copy_to_psum(i + 1, "top", 1)
            finish(i - 1, 0)
            combine(i, 1, weight, ALU.add, base_1)
            times_prob(nc.gpsimd, i, 1)
            if i + 3 < CHUNKS:
                load_prob(i + 3)
            regroup(i, 0)
            regroup(i, 1)
            column_sums(i)
            mark_top(i + 1, [top_0, top_1])
            finish(i - 1, 1)
            finish(i - 1, 2)
            start_gain(i + 1)
            finish(i - 1, 3)
            load_centre(i + 1)
            finish_gain(i + 1)
            if i == 0:
                quantise_x(2)
                quantise_x(3)
            quantise(i, 0)
            make_base(i + 1)
            make_bonus(i + 1)
            bonus_0, base_0, bonus_1 = (
                copy_to_psum(i + 1, "bonus", 0),
                copy_to_psum(i + 1, "base", 0),
                copy_to_psum(i + 1, "bonus", 1),
            )
            quantise(i, 1)
            products(i)

        last = CHUNKS - 1
        combine(last, 0, weight, ALU.mult, bonus_0)
        base_1 = copy_to_psum(last, "base", 1)
        combine(last, 1, weight, ALU.mult, bonus_1)
        combine(last, 0, weight, ALU.add, base_0)
        combine(last, 1, weight, ALU.add, base_1)
        for h in range(HALVES):
            times_prob(nc.vector, last, h)
            regroup(last, h)
        column_sums(last)
        for k in range(OUT_TILES):
            finish(last - 1, k)
        for h in range(HALVES):
            quantise(last, h)
        products(last)
        for k in range(OUT_TILES):
            finish(last, k)
